import numpy as np
import ml_dtypes

BF16 = ml_dtypes.bfloat16


def bf(x):
    return np.asarray(x, np.float32).astype(BF16)


def f32(x):
    return np.asarray(x, np.float32)


def f64(x):
    return np.asarray(x).astype(np.float64)


def striped(idx):
    return np.tile(idx.reshape(-1, 16).T, (8, 1))


S, D, M, B, T, K, N, TW, TP = 512, 128, 256, 32, 32, 3, 1024, 30, 15
SLOPE = 0.01


def setup_inputs():
    sc = 1.0 / np.sqrt(K * D)
    return {"table": bf(np.random.standard_normal((S, D))), "w0": bf(sc * np.random.standard_normal((D, M))), "w1": bf(sc * np.random.standard_normal((D, M))), "w2": bf(sc * np.random.standard_normal((D, M))), "bias": f32(0.1 * np.random.standard_normal((M, 1))), "offs": striped(np.random.permutation(np.tile(np.arange(S), 2))[:N])}


def reference(table, w0, w1, w2, bias, offs):
    idx = offs[:16].T.reshape(-1)
    x = f64(table)[idx].T
    y = f64(bias)[:, :, None]
    for t, w in enumerate((w0, w1, w2)):
        y = y + (f64(w).T @ x).reshape(M, B, T)[:, :, t:t + TW]
    y = np.maximum(y, SLOPE * y)
    return y.reshape(M, B, TP, TW // TP).max(axis=3).reshape(M, B * TP)

@@ -1,0 +1,95 @@
+import concourse.mybir as mybir
+from concourse.masks import make_identity
+
+BF16, F32, U16 = mybir.dt.bfloat16, mybir.dt.float32, mybir.dt.uint16
+ADD, MULT, MAX = mybir.AluOpType.add, mybir.AluOpType.mult, mybir.AluOpType.max
+IDENTITY = mybir.ActivationFunctionType.Identity
+
+P = 128
+WORDS, FEATURES = 512, 128
+OUT_FEATURES = 256
+ENTRIES = 1024
+SENTENCE = 32
+TAPS = 3
+POSITIONS = SENTENCE - TAPS + 1
+POOLED = POSITIONS // 2
+SLOPE = 0.01
+
+BLOCKS = WORDS // P
+HALVES = OUT_FEATURES // P
+PIECE = 512
+PIECES = ENTRIES // PIECE
+ROWS = PIECE // SENTENCE
+
+FLOPS = 2 * TAPS * FEATURES * OUT_FEATURES * ENTRIES
+
+
+def tile_matchcnn_st_kernel(tc, table, w0, w1, w2, bias, offs, out):
+    nc = tc.nc
+    with (
+        tc.tile_pool(name="held", bufs=1) as held,
+        tc.tile_pool(name="work", bufs=2) as work,
+        tc.psum_pool(name="flip", bufs=2) as flip,
+        tc.psum_pool(name="prod", bufs=2) as prod,
+    ):
+        offsets = held.tile([P, ENTRIES // 16], U16, name="offsets")
+        nc.sync.dma_start(offsets[:], offs)
+
+        rows = held.tile([P, BLOCKS, FEATURES], BF16, name="rows")
+        nc.sync.dma_start(rows[:], table.rearrange("(b p) k -> p b k", p=P))
+
+        taps = []
+        for t, w in enumerate((w0, w1, w2)):
+            tap = held.tile([FEATURES, OUT_FEATURES], BF16, name=f"tap{t}")
+            nc.scalar.dma_start(tap[:], w)
+            taps.append(tap)
+
+        bias_cols = []
+        for h in range(HALVES):
+            bias_col = held.tile([P, 1], F32, name=f"bias_col{h}")
+            nc.gpsimd.dma_start(bias_col[:], bias[h * P : (h + 1) * P, :])
+            bias_cols.append(bias_col)
+
+        identity = held.tile([P, P], BF16, name="identity")
+        make_identity(nc, identity[:])
+        words = held.tile([FEATURES, WORDS], BF16, name="words")
+        for b in range(BLOCKS):
+            flipped = flip.tile([FEATURES, P], BF16, name="flipped")
+            nc.tensor.transpose(flipped[:], rows[:, b, :], identity[:])
+            nc.vector.tensor_copy(words[:, b * P : (b + 1) * P], flipped[:])
+
+        for h in range(HALVES):
+            for c in range(PIECES):
+                piece = offsets[:, c * (PIECE // 16) : (c + 1) * (PIECE // 16)]
+
+                products = []
+                for t in range(TAPS):
+                    product = prod.tile([P, PIECE], F32, name=f"product{t}")
+                    nc.tensor.matmul(
+                        product[:],
+                        taps[t][:, h * P : (h + 1) * P],
+                        words[:].indirect(piece),
+                        start=True,
+                        stop=True,
+                    )
+                    products.append(product[:].rearrange("m (r i) -> m r i", i=SENTENCE))
+
+                conv = work.tile([P, ROWS, POSITIONS], F32, name="conv")
+                nc.scalar.activation(
+                    conv[:], products[0][:, :, 0:POSITIONS], IDENTITY, bias=bias_cols[h][:]
+                )
+                for t in range(1, TAPS):
+                    nc.vector.tensor_tensor(
+                        conv[:], products[t][:, :, t : t + POSITIONS], conv[:], ADD
+                    )
+
+                pairs = conv[:].rearrange("m r (q two) -> m r q two", two=2)
+                peak = work.tile([P, ROWS, POOLED], F32, name="peak")
+                nc.vector.tensor_tensor(peak[:], pairs[:, :, :, 0], pairs[:, :, :, 1], MAX)
+                pooled = work.tile([P, ROWS, POOLED], F32, name="pooled")
+                nc.vector.scalar_tensor_tensor(pooled[:], peak[:], SLOPE, peak[:], MULT, MAX)
+
+                nc.sync.dma_start(
+                    out[h * P : (h + 1) * P, c * ROWS * POOLED : (c + 1) * ROWS * POOLED],
+                    pooled[:].rearrange("m r q -> m (r q)"),
+                )

@@ -3,7 +3,6 @@ from concourse.masks import make_identity
 
 BF16, F32, U16 = mybir.dt.bfloat16, mybir.dt.float32, mybir.dt.uint16
 ADD, MULT, MAX = mybir.AluOpType.add, mybir.AluOpType.mult, mybir.AluOpType.max
-IDENTITY = mybir.ActivationFunctionType.Identity
 
 P = 128
 WORDS, FEATURES = 512, 128
@@ -20,6 +19,7 @@ HALVES = OUT_FEATURES // P
 PIECE = 512
 PIECES = ENTRIES // PIECE
 ROWS = PIECE // SENTENCE
+WARM_UPS = 2
 
 FLOPS = 2 * TAPS * FEATURES * OUT_FEATURES * ENTRIES
 
@@ -29,67 +29,95 @@ def tile_matchcnn_st_kernel(tc, table, w0, w1, w2, bias, offs, out):
     with (
         tc.tile_pool(name="held", bufs=1) as held,
         tc.tile_pool(name="work", bufs=2) as work,
-        tc.psum_pool(name="flip", bufs=2) as flip,
-        tc.psum_pool(name="prod", bufs=2) as prod,
     ):
+        rows = []
+        for a, queue in enumerate((nc.sync, nc.scalar)):
+            two_blocks = held.tile([P, BLOCKS // 2, FEATURES], BF16, name=f"rows{a}")
+            queue.dma_start(
+                two_blocks[:],
+                table[a * 2 * P : (a + 1) * 2 * P, :].rearrange("(b p) k -> p b k", p=P),
+            )
+            rows.append(two_blocks)
+
         offsets = held.tile([P, ENTRIES // 16], U16, name="offsets")
         nc.sync.dma_start(offsets[:], offs)
 
-        rows = held.tile([P, BLOCKS, FEATURES], BF16, name="rows")
-        nc.sync.dma_start(rows[:], table.rearrange("(b p) k -> p b k", p=P))
+        identity = held.tile([P, P], BF16, name="identity")
+        make_identity(nc, identity[:])
 
         taps = []
-        for t, w in enumerate((w0, w1, w2)):
+        for t, (w, queue) in enumerate(((w0, nc.scalar), (w1, nc.sync), (w2, nc.scalar))):
             tap = held.tile([FEATURES, OUT_FEATURES], BF16, name=f"tap{t}")
-            nc.scalar.dma_start(tap[:], w)
+            queue.dma_start(tap[:], w)
             taps.append(tap)
 
         bias_cols = []
-        for h in range(HALVES):
+        for h, queue in enumerate((nc.sync, nc.scalar)):
             bias_col = held.tile([P, 1], F32, name=f"bias_col{h}")
-            nc.gpsimd.dma_start(bias_col[:], bias[h * P : (h + 1) * P, :])
+            queue.dma_start(bias_col[:], bias[h * P : (h + 1) * P, :])
             bias_cols.append(bias_col)
 
-        identity = held.tile([P, P], BF16, name="identity")
-        make_identity(nc, identity[:])
         words = held.tile([FEATURES, WORDS], BF16, name="words")
-        for b in range(BLOCKS):
-            flipped = flip.tile([FEATURES, P], BF16, name="flipped")
-            nc.tensor.transpose(flipped[:], rows[:, b, :], identity[:])
-            nc.vector.tensor_copy(words[:, b * P : (b + 1) * P], flipped[:])
+        with tc.psum_pool(name="early", bufs=2) as early:
+            zeros = held.tile([P, PIECE], BF16, name="zeros")
+            nc.vector.memset(zeros[:], 0.0)
+            for i in range(WARM_UPS):
+                unused = early.tile([P, PIECE], F32, name="unused")
+                nc.tensor.matmul(unused[:], zeros[:, 0:P], zeros[:], start=True, stop=True)
 
-        for h in range(HALVES):
+            for s in range(BLOCKS):
+                flipped = early.tile([FEATURES, P], BF16, name="flipped")
+                nc.tensor.transpose(flipped[:], rows[s // 2][:, s % 2, :], identity[:])
+                nc.vector.tensor_copy(words[:, s * P : (s + 1) * P], flipped[:])
+
+        halves = range(HALVES)
+        with tc.psum_pool(name="prod", bufs=1) as prod:
             for c in range(PIECES):
                 piece = offsets[:, c * (PIECE // 16) : (c + 1) * (PIECE // 16)]
 
                 products = []
                 for t in range(TAPS):
-                    product = prod.tile([P, PIECE], F32, name=f"product{t}")
-                    nc.tensor.matmul(
-                        product[:],
-                        taps[t][:, h * P : (h + 1) * P],
-                        words[:].indirect(piece),
-                        start=True,
-                        stop=True,
-                    )
-                    products.append(product[:].rearrange("m (r i) -> m r i", i=SENTENCE))
+                    products.append([])
+                    for h in halves:
+                        product = prod.tile([P, PIECE], F32, name=f"product{t}{h}")
+                        nc.tensor.matmul(
+                            product[:],
+                            taps[t][:, h * P : (h + 1) * P],
+                            words[:].indirect(piece),
+                            start=True,
+                            stop=True,
+                        )
+                        products[t].append(product[:].rearrange("m (r i) -> m r i", i=SENTENCE))
 
-                conv = work.tile([P, ROWS, POSITIONS], F32, name="conv")
-                nc.scalar.activation(
-                    conv[:], products[0][:, :, 0:POSITIONS], IDENTITY, bias=bias_cols[h][:]
-                )
-                for t in range(1, TAPS):
+                convs = [work.tile([P, ROWS, POSITIONS], F32, name=f"conv{h}") for h in halves]
+                for h in halves:
+                    nc.scalar.copy(convs[h][:], products[0][h][:, :, 0:POSITIONS])
+                for h in halves:
                     nc.vector.tensor_tensor(
-                        conv[:], products[t][:, :, t : t + POSITIONS], conv[:], ADD
+                        convs[h][:], products[1][h][:, :, 1 : 1 + POSITIONS], convs[h][:], ADD
+                    )
+                for h in halves:
+                    nc.vector.scalar_tensor_tensor(
+                        convs[h][:],
+                        products[2][h][:, :, 2 : 2 + POSITIONS],
+                        bias_cols[h][:],
+                        convs[h][:],
+                        ADD,
+                        ADD,
                     )
 
-                pairs = conv[:].rearrange("m r (q two) -> m r q two", two=2)
-                peak = work.tile([P, ROWS, POOLED], F32, name="peak")
-                nc.vector.tensor_tensor(peak[:], pairs[:, :, :, 0], pairs[:, :, :, 1], MAX)
-                pooled = work.tile([P, ROWS, POOLED], F32, name="pooled")
-                nc.vector.scalar_tensor_tensor(pooled[:], peak[:], SLOPE, peak[:], MULT, MAX)
+                peaks = [work.tile([P, ROWS, POOLED], F32, name=f"peak{h}") for h in halves]
+                for h in halves:
+                    pairs = convs[h][:].rearrange("m r (q two) -> m r q two", two=2)
+                    nc.vector.tensor_tensor(peaks[h][:], pairs[:, :, :, 0], pairs[:, :, :, 1], MAX)
+                pooleds = [work.tile([P, ROWS, POOLED], F32, name=f"pooled{h}") for h in halves]
+                for h in halves:
+                    nc.vector.scalar_tensor_tensor(
+                        pooleds[h][:], peaks[h][:], SLOPE, peaks[h][:], MULT, MAX
+                    )
 
-                nc.sync.dma_start(
-                    out[h * P : (h + 1) * P, c * ROWS * POOLED : (c + 1) * ROWS * POOLED],
-                    pooled[:].rearrange("m r q -> m (r q)"),
-                )
+                for h, queue in zip(halves, (nc.sync, nc.scalar)):
+                    queue.dma_start(
+                        out[h * P : (h + 1) * P, c * ROWS * POOLED : (c + 1) * ROWS * POOLED],
+                        pooleds[h][:].rearrange("m r q -> m (r q)"),
+                    )

@@ -19,7 +19,6 @@ HALVES = OUT_FEATURES // P
 PIECE = 512
 PIECES = ENTRIES // PIECE
 ROWS = PIECE // SENTENCE
-WARM_UPS = 2
 
 FLOPS = 2 * TAPS * FEATURES * OUT_FEATURES * ENTRIES
 
@@ -59,12 +58,6 @@ def tile_matchcnn_st_kernel(tc, table, w0, w1, w2, bias, offs, out):
 
         words = held.tile([FEATURES, WORDS], BF16, name="words")
         with tc.psum_pool(name="early", bufs=2) as early:
-            zeros = held.tile([P, PIECE], BF16, name="zeros")
-            nc.vector.memset(zeros[:], 0.0)
-            for i in range(WARM_UPS):
-                unused = early.tile([P, PIECE], F32, name="unused")
-                nc.tensor.matmul(unused[:], zeros[:, 0:P], zeros[:], start=True, stop=True)
-
             for s in range(BLOCKS):
                 flipped = early.tile([FEATURES, P], BF16, name="flipped")
                 nc.tensor.transpose(flipped[:], rows[s // 2][:, s % 2, :], identity[:])

@@ -19,6 +19,7 @@ HALVES = OUT_FEATURES // P
 PIECE = 512
 PIECES = ENTRIES // PIECE
 ROWS = PIECE // SENTENCE
+WARM_UPS = 4
 
 FLOPS = 2 * TAPS * FEATURES * OUT_FEATURES * ENTRIES
 
@@ -58,6 +59,12 @@ def tile_matchcnn_st_kernel(tc, table, w0, w1, w2, bias, offs, out):
 
         words = held.tile([FEATURES, WORDS], BF16, name="words")
         with tc.psum_pool(name="early", bufs=2) as early:
+            zeros = held.tile([P, PIECE], BF16, name="zeros")
+            nc.vector.memset(zeros[:], 0.0)
+            for i in range(WARM_UPS):
+                unused = early.tile([P, PIECE], F32, name="unused")
+                nc.tensor.matmul(unused[:], zeros[:, 0:P], zeros[:], start=True, stop=True)
+
             for s in range(BLOCKS):
                 flipped = early.tile([FEATURES, P], BF16, name="flipped")
                 nc.tensor.transpose(flipped[:], rows[s // 2][:, s % 2, :], identity[:])

@@ -19,7 +19,6 @@ HALVES = OUT_FEATURES // P
 PIECE = 512
 PIECES = ENTRIES // PIECE
 ROWS = PIECE // SENTENCE
-WARM_UPS = 4
 
 FLOPS = 2 * TAPS * FEATURES * OUT_FEATURES * ENTRIES
 
@@ -58,15 +57,9 @@ def tile_matchcnn_st_kernel(tc, table, w0, w1, w2, bias, offs, out):
             bias_cols.append(bias_col)
 
         words = held.tile([FEATURES, WORDS], BF16, name="words")
-        with tc.psum_pool(name="early", bufs=2) as early:
-            zeros = held.tile([P, PIECE], BF16, name="zeros")
-            nc.vector.memset(zeros[:], 0.0)
-            for i in range(WARM_UPS):
-                unused = early.tile([P, PIECE], F32, name="unused")
-                nc.tensor.matmul(unused[:], zeros[:, 0:P], zeros[:], start=True, stop=True)
-
+        with tc.psum_pool(name="flip", bufs=BLOCKS) as flip:
             for s in range(BLOCKS):
-                flipped = early.tile([FEATURES, P], BF16, name="flipped")
+                flipped = flip.tile([FEATURES, P], BF16, name="flipped")
                 nc.tensor.transpose(flipped[:], rows[s // 2][:, s % 2, :], identity[:])
                 nc.vector.tensor_copy(words[:, s * P : (s + 1) * P], flipped[:])
 

@@ -3,6 +3,7 @@ from concourse.masks import make_identity
 
 BF16, F32, U16 = mybir.dt.bfloat16, mybir.dt.float32, mybir.dt.uint16
 ADD, MULT, MAX = mybir.AluOpType.add, mybir.AluOpType.mult, mybir.AluOpType.max
+IDENTITY = mybir.ActivationFunctionType.Identity
 
 P = 128
 WORDS, FEATURES = 512, 128
@@ -84,20 +85,14 @@ def tile_matchcnn_st_kernel(tc, table, w0, w1, w2, bias, offs, out):
 
                 convs = [work.tile([P, ROWS, POSITIONS], F32, name=f"conv{h}") for h in halves]
                 for h in halves:
-                    nc.scalar.copy(convs[h][:], products[0][h][:, :, 0:POSITIONS])
-                for h in halves:
-                    nc.vector.tensor_tensor(
-                        convs[h][:], products[1][h][:, :, 1 : 1 + POSITIONS], convs[h][:], ADD
+                    nc.scalar.activation(
+                        convs[h][:], products[0][h][:, :, 0:POSITIONS], IDENTITY, bias=bias_cols[h][:]
                     )
-                for h in halves:
-                    nc.vector.scalar_tensor_tensor(
-                        convs[h][:],
-                        products[2][h][:, :, 2 : 2 + POSITIONS],
-                        bias_cols[h][:],
-                        convs[h][:],
-                        ADD,
-                        ADD,
-                    )
+                for t in range(1, TAPS):
+                    for h in halves:
+                        nc.vector.tensor_tensor(
+                            convs[h][:], products[t][h][:, :, t : t + POSITIONS], convs[h][:], ADD
+                        )
 
                 peaks = [work.tile([P, ROWS, POOLED], F32, name=f"peak{h}") for h in halves]
                 for h in halves:

@@ -16,7 +16,6 @@ POOLED = POSITIONS // 2
 SLOPE = 0.01
 
 BLOCKS = WORDS // P
-HALVES = OUT_FEATURES // P
 PIECE = 512
 PIECES = ENTRIES // PIECE
 ROWS = PIECE // SENTENCE
@@ -64,48 +63,55 @@ def tile_matchcnn_st_kernel(tc, table, w0, w1, w2, bias, offs, out):
                 nc.tensor.transpose(flipped[:], rows[s // 2][:, s % 2, :], identity[:])
                 nc.vector.tensor_copy(words[:, s * P : (s + 1) * P], flipped[:])
 
-        halves = range(HALVES)
-        with tc.psum_pool(name="prod", bufs=1) as prod:
+        with tc.psum_pool(name="sums", bufs=2) as sums:
             for c in range(PIECES):
-                piece = offsets[:, c * (PIECE // 16) : (c + 1) * (PIECE // 16)]
+                first = c * (PIECE // 16)
+                middle = first + PIECE // 32
+                last = first + PIECE // 16
+                for h, queue in enumerate((nc.sync, nc.scalar)):
+                    features = slice(h * P, (h + 1) * P)
+                    early = sums.tile([P, PIECE], F32, name="early")
+                    nc.tensor.matmul(
+                        early[:], taps[0][:, features], words[:].indirect(offsets[:, first:last]),
+                        start=True, stop=False,
+                    )
+                    nc.tensor.matmul(
+                        early[:, PIECE // 2 - 1 : PIECE - 1], taps[1][:, features],
+                        words[:].indirect(offsets[:, middle:last]),
+                        start=False, stop=True,
+                    )
+                    late = sums.tile([P, PIECE], F32, name="late")
+                    nc.tensor.matmul(
+                        late[:], taps[2][:, features], words[:].indirect(offsets[:, first:last]),
+                        start=True, stop=False,
+                    )
+                    nc.tensor.matmul(
+                        late[:, 1 : PIECE // 2 + 1], taps[1][:, features],
+                        words[:].indirect(offsets[:, first:middle]),
+                        start=False, stop=True,
+                    )
 
-                products = []
-                for t in range(TAPS):
-                    products.append([])
-                    for h in halves:
-                        product = prod.tile([P, PIECE], F32, name=f"product{t}{h}")
-                        nc.tensor.matmul(
-                            product[:],
-                            taps[t][:, h * P : (h + 1) * P],
-                            words[:].indirect(piece),
-                            start=True,
-                            stop=True,
-                        )
-                        products[t].append(product[:].rearrange("m (r i) -> m r i", i=SENTENCE))
-
-                convs = [work.tile([P, ROWS, POSITIONS], F32, name=f"conv{h}") for h in halves]
-                for h in halves:
+                    conv = work.tile([P, ROWS, POSITIONS], F32, name="conv")
                     nc.scalar.activation(
-                        convs[h][:], products[0][h][:, :, 0:POSITIONS], IDENTITY, bias=bias_cols[h][:]
+                        conv[:],
+                        early[:].rearrange("m (r i) -> m r i", i=SENTENCE)[:, :, 0:POSITIONS],
+                        IDENTITY,
+                        bias=bias_cols[h][:],
                     )
-                for t in range(1, TAPS):
-                    for h in halves:
-                        nc.vector.tensor_tensor(
-                            convs[h][:], products[t][h][:, :, t : t + POSITIONS], convs[h][:], ADD
-                        )
-
-                peaks = [work.tile([P, ROWS, POOLED], F32, name=f"peak{h}") for h in halves]
-                for h in halves:
-                    pairs = convs[h][:].rearrange("m r (q two) -> m r q two", two=2)
-                    nc.vector.tensor_tensor(peaks[h][:], pairs[:, :, :, 0], pairs[:, :, :, 1], MAX)
-                pooleds = [work.tile([P, ROWS, POOLED], F32, name=f"pooled{h}") for h in halves]
-                for h in halves:
-                    nc.vector.scalar_tensor_tensor(
-                        pooleds[h][:], peaks[h][:], SLOPE, peaks[h][:], MULT, MAX
+                    nc.vector.tensor_tensor(
+                        conv[:],
+                        late[:].rearrange("m (r i) -> m r i", i=SENTENCE)[:, :, TAPS - 1 : SENTENCE],
+                        conv[:],
+                        ADD,
                     )
 
-                for h, queue in zip(halves, (nc.sync, nc.scalar)):
+                    pairs = conv[:].rearrange("m r (q two) -> m r q two", two=2)
+                    peak = work.tile([P, ROWS, POOLED], F32, name="peak")
+                    nc.vector.tensor_tensor(peak[:], pairs[:, :, :, 0], pairs[:, :, :, 1], MAX)
+                    pooled = work.tile([P, ROWS, POOLED], F32, name="pooled")
+                    nc.vector.scalar_tensor_tensor(pooled[:], peak[:], SLOPE, peak[:], MULT, MAX)
+
                     queue.dma_start(
-                        out[h * P : (h + 1) * P, c * ROWS * POOLED : (c + 1) * ROWS * POOLED],
-                        pooleds[h][:].rearrange("m r q -> m (r q)"),
+                        out[features, c * ROWS * POOLED : (c + 1) * ROWS * POOLED],
+                        pooled[:].rearrange("m r q -> m (r q)"),
                     )

@@ -19,6 +19,7 @@ BLOCKS = WORDS // P
 PIECE = 512
 PIECES = ENTRIES // PIECE
 ROWS = PIECE // SENTENCE
+UNITS = PIECES * (OUT_FEATURES // P)
 
 FLOPS = 2 * TAPS * FEATURES * OUT_FEATURES * ENTRIES
 
@@ -27,7 +28,7 @@ def tile_matchcnn_st_kernel(tc, table, w0, w1, w2, bias, offs, out):
     nc = tc.nc
     with (
         tc.tile_pool(name="held", bufs=1) as held,
-        tc.tile_pool(name="work", bufs=2) as work,
+        tc.tile_pool(name="work", bufs=UNITS) as work,
     ):
         rows = []
         for a, queue in enumerate((nc.sync, nc.scalar)):
@@ -68,7 +69,7 @@ def tile_matchcnn_st_kernel(tc, table, w0, w1, w2, bias, offs, out):
                 first = c * (PIECE // 16)
                 middle = first + PIECE // 32
                 last = first + PIECE // 16
-                for h, queue in enumerate((nc.sync, nc.scalar)):
+                for h in range(OUT_FEATURES // P):
                     features = slice(h * P, (h + 1) * P)
                     early = sums.tile([P, PIECE], F32, name="early")
                     nc.tensor.matmul(
@@ -111,7 +112,7 @@ def tile_matchcnn_st_kernel(tc, table, w0, w1, w2, bias, offs, out):
                     pooled = work.tile([P, ROWS, POOLED], F32, name="pooled")
                     nc.vector.scalar_tensor_tensor(pooled[:], peak[:], SLOPE, peak[:], MULT, MAX)
 
-                    queue.dma_start(
+                    nc.sync.dma_start(
                         out[features, c * ROWS * POOLED : (c + 1) * ROWS * POOLED],
                         pooled[:].rearrange("m r q -> m (r q)"),
                     )

@@ -19,6 +19,8 @@ BLOCKS = WORDS // P
 PIECE = 512
 PIECES = ENTRIES // PIECE
 ROWS = PIECE // SENTENCE
+GROUPS = 2
+GROUP_ROWS = ROWS // GROUPS
 UNITS = PIECES * (OUT_FEATURES // P)
 
 FLOPS = 2 * TAPS * FEATURES * OUT_FEATURES * ENTRIES
@@ -99,20 +101,27 @@ def tile_matchcnn_st_kernel(tc, table, w0, w1, w2, bias, offs, out):
                         IDENTITY,
                         bias=bias_cols[h][:],
                     )
-                    nc.vector.tensor_tensor(
-                        conv[:],
-                        late[:].rearrange("m (r i) -> m r i", i=SENTENCE)[:, :, TAPS - 1 : SENTENCE],
-                        conv[:],
-                        ADD,
-                    )
 
-                    pairs = conv[:].rearrange("m r (q two) -> m r q two", two=2)
-                    peak = work.tile([P, ROWS, POOLED], F32, name="peak")
-                    nc.vector.tensor_tensor(peak[:], pairs[:, :, :, 0], pairs[:, :, :, 1], MAX)
-                    pooled = work.tile([P, ROWS, POOLED], F32, name="pooled")
-                    nc.vector.scalar_tensor_tensor(pooled[:], peak[:], SLOPE, peak[:], MULT, MAX)
+                    groups = range(GROUPS)
+                    shifted = late[:].rearrange("m (r i) -> m r i", i=SENTENCE)[:, :, TAPS - 1 : SENTENCE]
+                    totals = [work.tile([P, GROUP_ROWS, POSITIONS], F32, name=f"total{g}") for g in groups]
+                    for g in groups:
+                        rows_g = slice(g * GROUP_ROWS, (g + 1) * GROUP_ROWS)
+                        nc.vector.tensor_tensor(totals[g][:], shifted[:, rows_g, :], conv[:, rows_g, :], ADD)
 
-                    nc.sync.dma_start(
-                        out[features, c * ROWS * POOLED : (c + 1) * ROWS * POOLED],
-                        pooled[:].rearrange("m r q -> m (r q)"),
-                    )
+                    peaks = [work.tile([P, GROUP_ROWS, POOLED], F32, name=f"peak{g}") for g in groups]
+                    for g in groups:
+                        pairs = totals[g][:].rearrange("m r (q two) -> m r q two", two=2)
+                        nc.vector.tensor_tensor(peaks[g][:], pairs[:, :, :, 0], pairs[:, :, :, 1], MAX)
+                    pooleds = [work.tile([P, GROUP_ROWS, POOLED], F32, name=f"pooled{g}") for g in groups]
+                    for g in groups:
+                        nc.vector.scalar_tensor_tensor(
+                            pooleds[g][:], peaks[g][:], SLOPE, peaks[g][:], MULT, MAX
+                        )
+
+                    for g in groups:
+                        column = (c * ROWS + g * GROUP_ROWS) * POOLED
+                        nc.sync.dma_start(
+                            out[features, column : column + GROUP_ROWS * POOLED],
+                            pooleds[g][:].rearrange("m r q -> m (r q)"),
+                        )

@@ -67,6 +67,7 @@ def tile_matchcnn_st_kernel(tc, table, w0, w1, w2, bias, offs, out):
                 nc.vector.tensor_copy(words[:, s * P : (s + 1) * P], flipped[:])
 
         with tc.psum_pool(name="sums", bufs=2) as sums:
+            waiting_store = None
             for c in range(PIECES):
                 first = c * (PIECE // 16)
                 middle = first + PIECE // 32
@@ -101,6 +102,8 @@ def tile_matchcnn_st_kernel(tc, table, w0, w1, w2, bias, offs, out):
                         IDENTITY,
                         bias=bias_cols[h][:],
                     )
+                    if waiting_store is not None:
+                        nc.scalar.dma_start(*waiting_store)
 
                     groups = range(GROUPS)
                     shifted = late[:].rearrange("m (r i) -> m r i", i=SENTENCE)[:, :, TAPS - 1 : SENTENCE]
@@ -119,9 +122,15 @@ def tile_matchcnn_st_kernel(tc, table, w0, w1, w2, bias, offs, out):
                             pooleds[g][:], peaks[g][:], SLOPE, peaks[g][:], MULT, MAX
                         )
 
+                    stores = []
                     for g in groups:
                         column = (c * ROWS + g * GROUP_ROWS) * POOLED
-                        nc.sync.dma_start(
-                            out[features, column : column + GROUP_ROWS * POOLED],
-                            pooleds[g][:].rearrange("m r q -> m (r q)"),
+                        stores.append(
+                            (
+                                out[features, column : column + GROUP_ROWS * POOLED],
+                                pooleds[g][:].rearrange("m r q -> m (r q)"),
+                            )
                         )
+                    nc.sync.dma_start(*stores[0])
+                    waiting_store = stores[1]
+            nc.scalar.dma_start(*waiting_store)

@@ -21,7 +21,10 @@ PIECES = ENTRIES // PIECE
 ROWS = PIECE // SENTENCE
 GROUPS = 2
 GROUP_ROWS = ROWS // GROUPS
-UNITS = PIECES * (OUT_FEATURES // P)
+GROUP = PIECE // GROUPS
+HALVES = OUT_FEATURES // P
+UNITS = PIECES * HALVES
+PLAIN_UNIT = 1
 
 FLOPS = 2 * TAPS * FEATURES * OUT_FEATURES * ENTRIES
 
@@ -59,6 +62,11 @@ def tile_matchcnn_st_kernel(tc, table, w0, w1, w2, bias, offs, out):
             queue.dma_start(bias_col[:], bias[h * P : (h + 1) * P, :])
             bias_cols.append(bias_col)
 
+        zero = held.tile([P, 1], F32, name="zero")
+        idle = held.tile([P, 1], F32, name="idle")
+        nc.vector.memset(zero[:], 0.0)
+        nc.scalar.activation(idle[:], zero[:], IDENTITY)
+
         words = held.tile([FEATURES, WORDS], BF16, name="words")
         with tc.psum_pool(name="flip", bufs=BLOCKS) as flip:
             for s in range(BLOCKS):
@@ -66,71 +74,85 @@ def tile_matchcnn_st_kernel(tc, table, w0, w1, w2, bias, offs, out):
                 nc.tensor.transpose(flipped[:], rows[s // 2][:, s % 2, :], identity[:])
                 nc.vector.tensor_copy(words[:, s * P : (s + 1) * P], flipped[:])
 
-        with tc.psum_pool(name="sums", bufs=2) as sums:
-            waiting_store = None
-            for c in range(PIECES):
-                first = c * (PIECE // 16)
-                middle = first + PIECE // 32
-                last = first + PIECE // 16
-                for h in range(OUT_FEATURES // P):
-                    features = slice(h * P, (h + 1) * P)
-                    early = sums.tile([P, PIECE], F32, name="early")
-                    nc.tensor.matmul(
-                        early[:], taps[0][:, features], words[:].indirect(offsets[:, first:last]),
-                        start=True, stop=False,
-                    )
-                    nc.tensor.matmul(
-                        early[:, PIECE // 2 - 1 : PIECE - 1], taps[1][:, features],
-                        words[:].indirect(offsets[:, middle:last]),
-                        start=False, stop=True,
-                    )
-                    late = sums.tile([P, PIECE], F32, name="late")
-                    nc.tensor.matmul(
-                        late[:], taps[2][:, features], words[:].indirect(offsets[:, first:last]),
-                        start=True, stop=False,
-                    )
-                    nc.tensor.matmul(
-                        late[:, 1 : PIECE // 2 + 1], taps[1][:, features],
-                        words[:].indirect(offsets[:, first:middle]),
-                        start=False, stop=True,
+        def by_sentence(bank, tap):
+            return bank[:].rearrange("m (r i) -> m r i", i=SENTENCE)[:, :, tap : tap + POSITIONS]
+
+        with tc.psum_pool(name="sums", bufs=8) as sums:
+
+            def bank():
+                return sums.tile([P, PIECE], F32, name="bank")
+
+            def look_up(out_columns, tap, features, entry, count, start, stop):
+                nc.tensor.matmul(
+                    out_columns, taps[tap][:, features],
+                    words[:].indirect(offsets[:, entry // 16 : (entry + count) // 16]),
+                    start=start, stop=stop,
+                )
+
+            def pool_and_store(totals, features, rows, queues):
+                peaks = [work.tile([P, GROUP_ROWS, POOLED], F32, name=f"peak{g}") for g in range(len(totals))]
+                for total, peak in zip(totals, peaks):
+                    pairs = total[:].rearrange("m r (q two) -> m r q two", two=2)
+                    nc.vector.tensor_tensor(peak[:], pairs[:, :, :, 0], pairs[:, :, :, 1], MAX)
+                pooleds = [work.tile([P, GROUP_ROWS, POOLED], F32, name=f"pooled{g}") for g in range(len(totals))]
+                for peak, pooled in zip(peaks, pooleds):
+                    nc.vector.scalar_tensor_tensor(pooled[:], peak[:], SLOPE, peak[:], MULT, MAX)
+                for pooled, row, queue in zip(pooleds, rows, queues):
+                    queue.dma_start(
+                        out[features, row * POOLED : (row + GROUP_ROWS) * POOLED],
+                        pooled[:].rearrange("m r q -> m (r q)"),
                     )
 
+            groups = [slice(g * GROUP_ROWS, (g + 1) * GROUP_ROWS) for g in range(GROUPS)]
+            for u in range(UNITS):
+                c, h = u // HALVES, u % HALVES
+                first = c * PIECE
+                middle = first + GROUP
+                features = slice(h * P, (h + 1) * P)
+                plain, last = u == PLAIN_UNIT, u == UNITS - 1
+
+                early = bank()
+                look_up(early[:], 0, features, first, PIECE, start=True, stop=plain)
+                if plain:
+                    tap1 = bank()
+                    look_up(tap1[:], 1, features, first, PIECE, start=True, stop=True)
+                else:
+                    look_up(early[:, GROUP - 1 : PIECE - 1], 1, features, middle, GROUP, start=False, stop=True)
+
+                if last:
+                    late_b = bank()
+                    look_up(late_b[:, 0:GROUP], 2, features, middle, GROUP, start=True, stop=True)
+                    late_a = bank()
+                    look_up(late_a[:, 0 : GROUP + SENTENCE], 2, features, first, GROUP + SENTENCE, start=True, stop=False)
+                    look_up(late_a[:, 1 : GROUP + 1], 1, features, first, GROUP, start=False, stop=True)
+                else:
+                    late = bank()
+                    look_up(late[:], 2, features, first, PIECE, start=True, stop=plain)
+                    if not plain:
+                        look_up(late[:, 1 : GROUP + 1], 1, features, first, GROUP, start=False, stop=True)
+
+                early_positions = by_sentence(early, 0)
+                if last:
+                    convs = [work.tile([P, GROUP_ROWS, POSITIONS], F32, name=f"conv{g}") for g in range(GROUPS)]
+                    lates = [by_sentence(late_g, 2)[:, 0:GROUP_ROWS, :] for late_g in (late_a, late_b)]
+                    for g in (1, 0):
+                        nc.scalar.activation(convs[g][:], early_positions[:, groups[g], :], IDENTITY, bias=bias_cols[h][:])
+                    for g, queue in ((1, nc.scalar), (0, nc.sync)):
+                        total = work.tile([P, GROUP_ROWS, POSITIONS], F32, name=f"total{g}")
+                        nc.vector.tensor_tensor(total[:], lates[g], convs[g][:], ADD)
+                        pool_and_store([total], features, [c * ROWS + g * GROUP_ROWS], [queue])
+                else:
                     conv = work.tile([P, ROWS, POSITIONS], F32, name="conv")
-                    nc.scalar.activation(
-                        conv[:],
-                        early[:].rearrange("m (r i) -> m r i", i=SENTENCE)[:, :, 0:POSITIONS],
-                        IDENTITY,
-                        bias=bias_cols[h][:],
+                    nc.scalar.activation(conv[:], early_positions, IDENTITY, bias=bias_cols[h][:])
+                    parts = [conv[:, rows_g, :] for rows_g in groups]
+                    if plain:
+                        middles = [work.tile([P, GROUP_ROWS, POSITIONS], F32, name=f"middle{g}") for g in range(GROUPS)]
+                        for g in range(GROUPS):
+                            nc.vector.tensor_tensor(middles[g][:], by_sentence(tap1, 1)[:, groups[g], :], parts[g], ADD)
+                        parts = [middle_g[:] for middle_g in middles]
+                    totals = [work.tile([P, GROUP_ROWS, POSITIONS], F32, name=f"total{g}") for g in range(GROUPS)]
+                    for g in range(GROUPS):
+                        nc.vector.tensor_tensor(totals[g][:], by_sentence(late, 2)[:, groups[g], :], parts[g], ADD)
+                    pool_and_store(
+                        totals, features, [c * ROWS + g * GROUP_ROWS for g in range(GROUPS)], [nc.sync, nc.sync]
                     )
-                    if waiting_store is not None:
-                        nc.scalar.dma_start(*waiting_store)
-
-                    groups = range(GROUPS)
-                    shifted = late[:].rearrange("m (r i) -> m r i", i=SENTENCE)[:, :, TAPS - 1 : SENTENCE]
-                    totals = [work.tile([P, GROUP_ROWS, POSITIONS], F32, name=f"total{g}") for g in groups]
-                    for g in groups:
-                        rows_g = slice(g * GROUP_ROWS, (g + 1) * GROUP_ROWS)
-                        nc.vector.tensor_tensor(totals[g][:], shifted[:, rows_g, :], conv[:, rows_g, :], ADD)
-
-                    peaks = [work.tile([P, GROUP_ROWS, POOLED], F32, name=f"peak{g}") for g in groups]
-                    for g in groups:
-                        pairs = totals[g][:].rearrange("m r (q two) -> m r q two", two=2)
-                        nc.vector.tensor_tensor(peaks[g][:], pairs[:, :, :, 0], pairs[:, :, :, 1], MAX)
-                    pooleds = [work.tile([P, GROUP_ROWS, POOLED], F32, name=f"pooled{g}") for g in groups]
-                    for g in groups:
-                        nc.vector.scalar_tensor_tensor(
-                            pooleds[g][:], peaks[g][:], SLOPE, peaks[g][:], MULT, MAX
-                        )
-
-                    stores = []
-                    for g in groups:
-                        column = (c * ROWS + g * GROUP_ROWS) * POOLED
-                        stores.append(
-                            (
-                                out[features, column : column + GROUP_ROWS * POOLED],
-                                pooleds[g][:].rearrange("m r q -> m (r q)"),
-                            )
-                        )
-                    nc.sync.dma_start(*stores[0])
-                    waiting_store = stores[1]
-            nc.scalar.dma_start(*waiting_store)

@@ -137,10 +137,14 @@ def tile_matchcnn_st_kernel(tc, table, w0, w1, w2, bias, offs, out):
                     lates = [by_sentence(late_g, 2)[:, 0:GROUP_ROWS, :] for late_g in (late_a, late_b)]
                     for g in (1, 0):
                         nc.scalar.activation(convs[g][:], early_positions[:, groups[g], :], IDENTITY, bias=bias_cols[h][:])
-                    for g, queue in ((1, nc.scalar), (0, nc.sync)):
+                    totals = []
+                    for g in (1, 0):
                         total = work.tile([P, GROUP_ROWS, POSITIONS], F32, name=f"total{g}")
                         nc.vector.tensor_tensor(total[:], lates[g], convs[g][:], ADD)
-                        pool_and_store([total], features, [c * ROWS + g * GROUP_ROWS], [queue])
+                        totals.append(total)
+                    pool_and_store(
+                        totals, features, [c * ROWS + g * GROUP_ROWS for g in (1, 0)], [nc.scalar, nc.sync]
+                    )
                 else:
                     conv = work.tile([P, ROWS, POSITIONS], F32, name="conv")
                     nc.scalar.activation(conv[:], early_positions, IDENTITY, bias=bias_cols[h][:])

@@ -143,7 +143,7 @@ def tile_matchcnn_st_kernel(tc, table, w0, w1, w2, bias, offs, out):
                         nc.vector.tensor_tensor(total[:], lates[g], convs[g][:], ADD)
                         totals.append(total)
                     pool_and_store(
-                        totals, features, [c * ROWS + g * GROUP_ROWS for g in (1, 0)], [nc.scalar, nc.sync]
+                        totals, features, [c * ROWS + g * GROUP_ROWS for g in (1, 0)], [nc.sync, nc.sync]
                     )
                 else:
                     conv = work.tile([P, ROWS, POSITIONS], F32, name="conv")

@@ -24,7 +24,7 @@ GROUP_ROWS = ROWS // GROUPS
 GROUP = PIECE // GROUPS
 HALVES = OUT_FEATURES // P
 UNITS = PIECES * HALVES
-PLAIN_UNIT = 1
+PLAIN_UNITS = (0, 1)
 
 FLOPS = 2 * TAPS * FEATURES * OUT_FEATURES * ENTRIES
 
@@ -109,19 +109,20 @@ def tile_matchcnn_st_kernel(tc, table, w0, w1, w2, bias, offs, out):
                 first = c * PIECE
                 middle = first + GROUP
                 features = slice(h * P, (h + 1) * P)
-                plain, last = u == PLAIN_UNIT, u == UNITS - 1
+                plain, last = u in PLAIN_UNITS, u == UNITS - 1
 
                 early = bank()
-                look_up(early[:], 0, features, first, PIECE, start=True, stop=plain)
+                look_up(early[:], 0, features, first, PIECE, start=True, stop=plain or last)
                 if plain:
                     tap1 = bank()
                     look_up(tap1[:], 1, features, first, PIECE, start=True, stop=True)
-                else:
+                elif not last:
                     look_up(early[:, GROUP - 1 : PIECE - 1], 1, features, middle, GROUP, start=False, stop=True)
 
                 if last:
                     late_b = bank()
-                    look_up(late_b[:, 0:GROUP], 2, features, middle, GROUP, start=True, stop=True)
+                    look_up(late_b[:, 0 : GROUP + SENTENCE], 1, features, middle - SENTENCE, GROUP + SENTENCE, start=True, stop=False)
+                    look_up(late_b[:, SENTENCE - 1 : SENTENCE - 1 + GROUP], 2, features, middle, GROUP, start=False, stop=True)
                     late_a = bank()
                     look_up(late_a[:, 0 : GROUP + SENTENCE], 2, features, first, GROUP + SENTENCE, start=True, stop=False)
                     look_up(late_a[:, 1 : GROUP + 1], 1, features, first, GROUP, start=False, stop=True)
@@ -134,7 +135,7 @@ def tile_matchcnn_st_kernel(tc, table, w0, w1, w2, bias, offs, out):
                 early_positions = by_sentence(early, 0)
                 if last:
                     convs = [work.tile([P, GROUP_ROWS, POSITIONS], F32, name=f"conv{g}") for g in range(GROUPS)]
-                    lates = [by_sentence(late_g, 2)[:, 0:GROUP_ROWS, :] for late_g in (late_a, late_b)]
+                    lates = [by_sentence(late_a, 2)[:, 0:GROUP_ROWS, :], by_sentence(late_b, 1)[:, 1 : 1 + GROUP_ROWS, :]]
                     for g in (1, 0):
                         nc.scalar.activation(convs[g][:], early_positions[:, groups[g], :], IDENTITY, bias=bias_cols[h][:])
                     totals = []

@@ -89,19 +89,29 @@ def tile_matchcnn_st_kernel(tc, table, w0, w1, w2, bias, offs, out):
                     start=start, stop=stop,
                 )
 
-            def pool_and_store(totals, features, rows, queues):
-                peaks = [work.tile([P, GROUP_ROWS, POOLED], F32, name=f"peak{g}") for g in range(len(totals))]
-                for total, peak in zip(totals, peaks):
-                    pairs = total[:].rearrange("m r (q two) -> m r q two", two=2)
-                    nc.vector.tensor_tensor(peak[:], pairs[:, :, :, 0], pairs[:, :, :, 1], MAX)
-                pooleds = [work.tile([P, GROUP_ROWS, POOLED], F32, name=f"pooled{g}") for g in range(len(totals))]
-                for peak, pooled in zip(peaks, pooleds):
-                    nc.vector.scalar_tensor_tensor(pooled[:], peak[:], SLOPE, peak[:], MULT, MAX)
-                for pooled, row, queue in zip(pooleds, rows, queues):
-                    queue.dma_start(
-                        out[features, row * POOLED : (row + GROUP_ROWS) * POOLED],
-                        pooled[:].rearrange("m r q -> m (r q)"),
-                    )
+            def move(positions, name, h):
+                moved = work.tile([P, positions.shape[1], positions.shape[2]], F32, name=name)
+                nc.scalar.activation(moved[:], positions, IDENTITY, bias=bias_cols[h][:])
+                return moved
+
+            def add(positions, part, name):
+                total = work.tile([P, GROUP_ROWS, POSITIONS], F32, name=name)
+                nc.vector.tensor_tensor(total[:], positions, part, ADD)
+                return total
+
+            def pool(total, name):
+                peak = work.tile([P, GROUP_ROWS, POOLED], F32, name=name)
+                pairs = total[:].rearrange("m r (q two) -> m r q two", two=2)
+                nc.vector.tensor_tensor(peak[:], pairs[:, :, :, 0], pairs[:, :, :, 1], MAX)
+                return peak
+
+            def relu_and_store(peak, name, features, row):
+                pooled = work.tile([P, GROUP_ROWS, POOLED], F32, name=name)
+                nc.vector.scalar_tensor_tensor(pooled[:], peak[:], SLOPE, peak[:], MULT, MAX)
+                nc.sync.dma_start(
+                    out[features, row * POOLED : (row + GROUP_ROWS) * POOLED],
+                    pooled[:].rearrange("m r q -> m (r q)"),
+                )
 
             groups = [slice(g * GROUP_ROWS, (g + 1) * GROUP_ROWS) for g in range(GROUPS)]
             for u in range(UNITS):
@@ -109,55 +119,58 @@ def tile_matchcnn_st_kernel(tc, table, w0, w1, w2, bias, offs, out):
                 first = c * PIECE
                 middle = first + GROUP
                 features = slice(h * P, (h + 1) * P)
-                plain, last = u in PLAIN_UNITS, u == UNITS - 1
 
-                early = bank()
-                look_up(early[:], 0, features, first, PIECE, start=True, stop=plain or last)
-                if plain:
-                    tap1 = bank()
-                    look_up(tap1[:], 1, features, first, PIECE, start=True, stop=True)
-                elif not last:
-                    look_up(early[:, GROUP - 1 : PIECE - 1], 1, features, middle, GROUP, start=False, stop=True)
-
-                if last:
-                    late_b = bank()
-                    look_up(late_b[:, 0 : GROUP + SENTENCE], 1, features, middle - SENTENCE, GROUP + SENTENCE, start=True, stop=False)
-                    look_up(late_b[:, SENTENCE - 1 : SENTENCE - 1 + GROUP], 2, features, middle, GROUP, start=False, stop=True)
-                    late_a = bank()
-                    look_up(late_a[:, 0 : GROUP + SENTENCE], 2, features, first, GROUP + SENTENCE, start=True, stop=False)
-                    look_up(late_a[:, 1 : GROUP + 1], 1, features, first, GROUP, start=False, stop=True)
-                else:
+                if u < UNITS - 1:
+                    plain = u in PLAIN_UNITS
+                    early = bank()
+                    look_up(early[:], 0, features, first, PIECE, start=True, stop=plain)
+                    if plain:
+                        between = bank()
+                        look_up(between[:], 1, features, first, PIECE, start=True, stop=True)
+                    else:
+                        look_up(early[:, GROUP - 1 : PIECE - 1], 1, features, middle, GROUP, start=False, stop=True)
                     late = bank()
                     look_up(late[:], 2, features, first, PIECE, start=True, stop=plain)
                     if not plain:
                         look_up(late[:, 1 : GROUP + 1], 1, features, first, GROUP, start=False, stop=True)
 
-                early_positions = by_sentence(early, 0)
-                if last:
-                    convs = [work.tile([P, GROUP_ROWS, POSITIONS], F32, name=f"conv{g}") for g in range(GROUPS)]
-                    lates = [by_sentence(late_a, 2)[:, 0:GROUP_ROWS, :], by_sentence(late_b, 1)[:, 1 : 1 + GROUP_ROWS, :]]
-                    for g in (1, 0):
-                        nc.scalar.activation(convs[g][:], early_positions[:, groups[g], :], IDENTITY, bias=bias_cols[h][:])
-                    totals = []
-                    for g in (1, 0):
-                        total = work.tile([P, GROUP_ROWS, POSITIONS], F32, name=f"total{g}")
-                        nc.vector.tensor_tensor(total[:], lates[g], convs[g][:], ADD)
-                        totals.append(total)
-                    pool_and_store(
-                        totals, features, [c * ROWS + g * GROUP_ROWS for g in (1, 0)], [nc.sync, nc.sync]
-                    )
-                else:
-                    conv = work.tile([P, ROWS, POSITIONS], F32, name="conv")
-                    nc.scalar.activation(conv[:], early_positions, IDENTITY, bias=bias_cols[h][:])
+                    conv = move(by_sentence(early, 0), "conv", h)
                     parts = [conv[:, rows_g, :] for rows_g in groups]
                     if plain:
-                        middles = [work.tile([P, GROUP_ROWS, POSITIONS], F32, name=f"middle{g}") for g in range(GROUPS)]
-                        for g in range(GROUPS):
-                            nc.vector.tensor_tensor(middles[g][:], by_sentence(tap1, 1)[:, groups[g], :], parts[g], ADD)
-                        parts = [middle_g[:] for middle_g in middles]
-                    totals = [work.tile([P, GROUP_ROWS, POSITIONS], F32, name=f"total{g}") for g in range(GROUPS)]
+                        parts = [
+                            add(by_sentence(between, 1)[:, groups[g], :], parts[g], f"middle{g}")[:]
+                            for g in range(GROUPS)
+                        ]
+                    totals = [
+                        add(by_sentence(late, 2)[:, groups[g], :], parts[g], f"total{g}") for g in range(GROUPS)
+                    ]
+                    peaks = [pool(totals[g], f"peak{g}") for g in range(GROUPS)]
                     for g in range(GROUPS):
-                        nc.vector.tensor_tensor(totals[g][:], by_sentence(late, 2)[:, groups[g], :], parts[g], ADD)
-                    pool_and_store(
-                        totals, features, [c * ROWS + g * GROUP_ROWS for g in range(GROUPS)], [nc.sync, nc.sync]
+                        relu_and_store(peaks[g], f"pooled{g}", features, c * ROWS + g * GROUP_ROWS)
+                else:
+                    second = bank()
+                    look_up(
+                        second[:, 0 : GROUP + SENTENCE], 0, features, middle - SENTENCE, GROUP + SENTENCE,
+                        start=True, stop=False,
                     )
+                    for tap in (1, 2):
+                        look_up(
+                            second[:, SENTENCE - tap : SENTENCE - tap + GROUP], tap, features, middle, GROUP,
+                            start=False, stop=tap == 2,
+                        )
+                    early = bank()
+                    look_up(early[:, 0:GROUP], 0, features, first, GROUP, start=True, stop=True)
+                    late = bank()
+                    look_up(late[:, 0 : GROUP + SENTENCE], 2, features, first, GROUP + SENTENCE, start=True, stop=False)
+                    look_up(late[:, 1 : GROUP + 1], 1, features, first, GROUP, start=False, stop=True)
+
+                    pairs = by_sentence(second, 0)[:, 1 : 1 + GROUP_ROWS, :].rearrange("m r (q two) -> m r q two", two=2)
+                    evens = move(pairs[:, :, :, 0], "evens", h)
+                    peak = work.tile([P, GROUP_ROWS, POOLED], F32, name="peak1")
+                    nc.vector.scalar_tensor_tensor(
+                        peak[:], pairs[:, :, :, 1], bias_cols[h][:], evens[:], ADD, MAX
+                    )
+                    relu_and_store(peak, "pooled1", features, c * ROWS + GROUP_ROWS)
+                    conv = move(by_sentence(early, 0)[:, 0:GROUP_ROWS, :], "conv_first", h)
+                    total = add(by_sentence(late, 2)[:, 0:GROUP_ROWS, :], conv[:], "total0")
+                    relu_and_store(pool(total, "peak0"), "pooled0", features, c * ROWS)

import concourse.mybir as mybir
from concourse.masks import make_identity

BF16, F32, U16 = mybir.dt.bfloat16, mybir.dt.float32, mybir.dt.uint16
ADD, MULT, MAX = mybir.AluOpType.add, mybir.AluOpType.mult, mybir.AluOpType.max
IDENTITY = mybir.ActivationFunctionType.Identity

P = 128
WORDS, FEATURES = 512, 128
OUT_FEATURES = 256
ENTRIES = 1024
SENTENCE = 32
TAPS = 3
POSITIONS = SENTENCE - TAPS + 1
POOLED = POSITIONS // 2
SLOPE = 0.01

BLOCKS = WORDS // P
PIECE = 512
PIECES = ENTRIES // PIECE
ROWS = PIECE // SENTENCE
GROUPS = 2
GROUP_ROWS = ROWS // GROUPS
GROUP = PIECE // GROUPS
HALVES = OUT_FEATURES // P
UNITS = PIECES * HALVES
PLAIN_UNITS = (0, 1)

FLOPS = 2 * TAPS * FEATURES * OUT_FEATURES * ENTRIES


def tile_matchcnn_st_kernel(tc, table, w0, w1, w2, bias, offs, out):
    nc = tc.nc
    with (
        tc.tile_pool(name="held", bufs=1) as held,
        tc.tile_pool(name="work", bufs=UNITS) as work,
    ):
        rows = []
        for a, queue in enumerate((nc.sync, nc.scalar)):
            two_blocks = held.tile([P, BLOCKS // 2, FEATURES], BF16, name=f"rows{a}")
            queue.dma_start(
                two_blocks[:],
                table[a * 2 * P : (a + 1) * 2 * P, :].rearrange("(b p) k -> p b k", p=P),
            )
            rows.append(two_blocks)

        offsets = held.tile([P, ENTRIES // 16], U16, name="offsets")
        nc.sync.dma_start(offsets[:], offs)

        identity = held.tile([P, P], BF16, name="identity")
        make_identity(nc, identity[:])

        taps = []
        for t, (w, queue) in enumerate(((w0, nc.scalar), (w1, nc.sync), (w2, nc.scalar))):
            tap = held.tile([FEATURES, OUT_FEATURES], BF16, name=f"tap{t}")
            queue.dma_start(tap[:], w)
            taps.append(tap)

        bias_cols = []
        for h, queue in enumerate((nc.sync, nc.scalar)):
            bias_col = held.tile([P, 1], F32, name=f"bias_col{h}")
            queue.dma_start(bias_col[:], bias[h * P : (h + 1) * P, :])
            bias_cols.append(bias_col)

        zero = held.tile([P, 1], F32, name="zero")
        idle = held.tile([P, 1], F32, name="idle")
        nc.vector.memset(zero[:], 0.0)
        nc.scalar.activation(idle[:], zero[:], IDENTITY)

        words = held.tile([FEATURES, WORDS], BF16, name="words")
        with tc.psum_pool(name="flip", bufs=BLOCKS) as flip:
            for s in range(BLOCKS):
                flipped = flip.tile([FEATURES, P], BF16, name="flipped")
                nc.tensor.transpose(flipped[:], rows[s // 2][:, s % 2, :], identity[:])
                nc.vector.tensor_copy(words[:, s * P : (s + 1) * P], flipped[:])

        def by_sentence(bank, tap):
            return bank[:].rearrange("m (r i) -> m r i", i=SENTENCE)[:, :, tap : tap + POSITIONS]

        with tc.psum_pool(name="sums", bufs=8) as sums:

            def bank():
                return sums.tile([P, PIECE], F32, name="bank")

            def look_up(out_columns, tap, features, entry, count, start, stop):
                nc.tensor.matmul(
                    out_columns, taps[tap][:, features],
                    words[:].indirect(offsets[:, entry // 16 : (entry + count) // 16]),
                    start=start, stop=stop,
                )

            def move(positions, name, h):
                moved = work.tile([P, positions.shape[1], positions.shape[2]], F32, name=name)
                nc.scalar.activation(moved[:], positions, IDENTITY, bias=bias_cols[h][:])
                return moved

            def add(positions, part, name):
                total = work.tile([P, GROUP_ROWS, POSITIONS], F32, name=name)
                nc.vector.tensor_tensor(total[:], positions, part, ADD)
                return total

            def pool(total, name):
                peak = work.tile([P, GROUP_ROWS, POOLED], F32, name=name)
                pairs = total[:].rearrange("m r (q two) -> m r q two", two=2)
                nc.vector.tensor_tensor(peak[:], pairs[:, :, :, 0], pairs[:, :, :, 1], MAX)
                return peak

            def relu_and_store(peak, name, features, row):
                pooled = work.tile([P, GROUP_ROWS, POOLED], F32, name=name)
                nc.vector.scalar_tensor_tensor(pooled[:], peak[:], SLOPE, peak[:], MULT, MAX)
                nc.sync.dma_start(
                    out[features, row * POOLED : (row + GROUP_ROWS) * POOLED],
                    pooled[:].rearrange("m r q -> m (r q)"),
                )

            groups = [slice(g * GROUP_ROWS, (g + 1) * GROUP_ROWS) for g in range(GROUPS)]
            for u in range(UNITS):
                c, h = u // HALVES, u % HALVES
                first = c * PIECE
                middle = first + GROUP
                features = slice(h * P, (h + 1) * P)

                if u < UNITS - 1:
                    plain = u in PLAIN_UNITS
                    early = bank()
                    look_up(early[:], 0, features, first, PIECE, start=True, stop=plain)
                    if plain:
                        between = bank()
                        look_up(between[:], 1, features, first, PIECE, start=True, stop=True)
                    else:
                        look_up(early[:, GROUP - 1 : PIECE - 1], 1, features, middle, GROUP, start=False, stop=True)
                    late = bank()
                    look_up(late[:], 2, features, first, PIECE, start=True, stop=plain)
                    if not plain:
                        look_up(late[:, 1 : GROUP + 1], 1, features, first, GROUP, start=False, stop=True)

                    conv = move(by_sentence(early, 0), "conv", h)
                    parts = [conv[:, rows_g, :] for rows_g in groups]
                    if plain:
                        parts = [
                            add(by_sentence(between, 1)[:, groups[g], :], parts[g], f"middle{g}")[:]
                            for g in range(GROUPS)
                        ]
                    totals = [
                        add(by_sentence(late, 2)[:, groups[g], :], parts[g], f"total{g}") for g in range(GROUPS)
                    ]
                    peaks = [pool(totals[g], f"peak{g}") for g in range(GROUPS)]
                    for g in range(GROUPS):
                        relu_and_store(peaks[g], f"pooled{g}", features, c * ROWS + g * GROUP_ROWS)
                else:
                    second = bank()
                    look_up(
                        second[:, 0 : GROUP + SENTENCE], 0, features, middle - SENTENCE, GROUP + SENTENCE,
                        start=True, stop=False,
                    )
                    for tap in (1, 2):
                        look_up(
                            second[:, SENTENCE - tap : SENTENCE - tap + GROUP], tap, features, middle, GROUP,
                            start=False, stop=tap == 2,
                        )
                    early = bank()
                    look_up(early[:, 0:GROUP], 0, features, first, GROUP, start=True, stop=True)
                    late = bank()
                    look_up(late[:, 0 : GROUP + SENTENCE], 2, features, first, GROUP + SENTENCE, start=True, stop=False)
                    look_up(late[:, 1 : GROUP + 1], 1, features, first, GROUP, start=False, stop=True)

                    pairs = by_sentence(second, 0)[:, 1 : 1 + GROUP_ROWS, :].rearrange("m r (q two) -> m r q two", two=2)
                    evens = move(pairs[:, :, :, 0], "evens", h)
                    peak = work.tile([P, GROUP_ROWS, POOLED], F32, name="peak1")
                    nc.vector.scalar_tensor_tensor(
                        peak[:], pairs[:, :, :, 1], bias_cols[h][:], evens[:], ADD, MAX
                    )
                    relu_and_store(peak, "pooled1", features, c * ROWS + GROUP_ROWS)
                    conv = move(by_sentence(early, 0)[:, 0:GROUP_ROWS, :], "conv_first", h)
                    total = add(by_sentence(late, 2)[:, 0:GROUP_ROWS, :], conv[:], "total0")
                    relu_and_store(pool(total, "peak0"), "pooled0", features, c * ROWS)
